import numpy as np
import ml_dtypes


def mxq(x, axis, fmt="e4m3"):
    dtype, down = {"e4m3": (ml_dtypes.float8_e4m3fn, 7), "e5m2": (ml_dtypes.float8_e5m2, 14)}[fmt]
    v = np.moveaxis(np.asarray(x, np.float32).astype(ml_dtypes.bfloat16).astype(np.float64), axis, -1)
    blocks = v.reshape(v.shape[:-1] + (-1, 32))
    amax = np.abs(blocks).max(-1, keepdims=True)
    byte = np.maximum(np.where(amax > 0, np.frexp(amax)[1] - 1 + 127, 0) - down, 1)
    scale = np.exp2(byte - 127.0)
    codes = (blocks / scale).astype(np.float32).astype(dtype).astype(np.float64)
    return np.moveaxis((codes * scale).reshape(v.shape), -1, axis)


WIDE = False


def mx_kscale(k):
    if not WIDE:
        return np.ones(k)
    levels = np.array([10, -10, 5, -5, 0])
    if k % 512:
        return np.exp2(np.random.permutation(np.resize(levels, k // 32))).repeat(32)
    a = np.empty((k // 512, 16))
    for p in range(k // 512):
        a[p, :8] = np.random.permutation(np.resize(levels, 8))
        for g in range(8):
            far = levels[np.abs(levels - a[p, g]) >= 10]
            a[p, g + 8] = far[np.random.randint(len(far))]
    return np.exp2(a.ravel()).repeat(32)


BF16 = ml_dtypes.bfloat16


def bf(x):
    return np.asarray(x, np.float32).astype(BF16)


def f64(x):
    return np.asarray(x).astype(np.float64)


B, S, K, H, D = 16, 384, 128, 512, 256
EPS = 1e-6


def setup_inputs():
    s = mx_kscale(H)
    rows = 0.5 * np.exp(0.5 * np.random.standard_normal((B, S, 1)))
    return {"hidden_states": bf(np.random.standard_normal((B, S, H)) * rows),
            "memory_state": bf(np.random.standard_normal((B, K, H)) * s),
            "q_w": bf(np.random.standard_normal((D, H)) * 1.5 / np.sqrt(H) / s),
            "k_w": bf(np.random.standard_normal((D, H)) * 1.5 / np.sqrt(H) / s),
            "norm_w": bf((1.0 + 0.3 * np.random.standard_normal(H)) * s)}


def reference(hidden_states, memory_state, q_w, k_w, norm_w):
    x = f64(hidden_states)
    normed = x * (1.0 / np.sqrt(np.mean(x * x, axis=-1, keepdims=True) + EPS)) * f64(norm_w)
    pool = np.concatenate([normed, f64(memory_state)], axis=1)
    pq = mxq(pool, 2, "e4m3")
    q = pq[:, :S] @ mxq(f64(q_w), 1, "e4m3").T
    k = pq @ mxq(f64(k_w), 1, "e4m3").T
    return q, k

@@ -1,0 +1,242 @@
+from contextlib import ExitStack
+
+import concourse.mybir as mybir
+from concourse.masks import make_identity
+
+F32 = mybir.dt.float32
+BF16 = mybir.dt.bfloat16
+U32 = mybir.dt.uint32
+U8 = mybir.dt.uint8
+FP8X4 = mybir.dt.float8_e4m3fn_x4
+ACT = mybir.ActivationFunctionType
+ALU = mybir.AluOpType
+
+P = 128
+PACK = 4
+B = 16
+S = 384
+H = 512
+D = 256
+EPS = 1e-6
+TOKEN_TILES = S // P
+POOL_TILES = TOKEN_TILES + 1
+MEMORY_LOAD = 4
+
+FLOPS = 2 * B * (S + S + P) * D * H
+
+SQUARES_AHEAD = 3
+SCALE_AHEAD = 2
+TURN_AHEAD = 1
+
+
+def tile_memresprojections_pa_t_kernel(
+    tc, hidden_states, memory_state, q_w, k_w, norm_w, out_0, out_1
+):
+    nc = tc.nc
+    with ExitStack() as ctx:
+        keep = ctx.enter_context(tc.tile_pool(name="keep", bufs=1))
+        stats = ctx.enter_context(tc.tile_pool(name="stats", bufs=4))
+        squares_pool = ctx.enter_context(tc.tile_pool(name="squares", bufs=4))
+        scaled_pool = ctx.enter_context(tc.tile_pool(name="scaled", bufs=2 * TOKEN_TILES))
+        grouped_pool = ctx.enter_context(tc.tile_pool(name="grouped", bufs=2))
+        mx_pool = ctx.enter_context(tc.tile_pool(name="mx", bufs=3))
+        result_pool = ctx.enter_context(tc.tile_pool(name="result", bufs=5))
+        turned_psum = ctx.enter_context(tc.psum_pool(name="turned", bufs=POOL_TILES))
+        acc_psum = ctx.enter_context(tc.psum_pool(name="acc", bufs=POOL_TILES))
+        ctx.enter_context(tc.manual_schedule())
+
+        eps = keep.tile([P, 1], F32)
+        nc.vector.memset(eps[:], EPS)
+        warm = keep.tile([P, 1], F32)
+        nc.scalar.activation(out=warm[:], in_=eps[:], func=ACT.Sqrt)
+        ident = keep.tile([P, P], F32)
+        make_identity(nc, ident[:])
+
+        x_all = keep.tile([P, B, TOKEN_TILES, H], BF16)
+        mem_all = keep.tile([P, B, H], BF16)
+        w_raw = keep.tile([P, 2, 2, H], BF16)
+        gain = keep.tile([P, PACK], BF16)
+
+        def load_hidden(b):
+            nc.sync.dma_start(
+                out=x_all[:, b], in_=hidden_states[b].rearrange("(p j) h -> p j h", j=TOKEN_TILES)
+            )
+
+        load_hidden(0)
+        nc.sync.dma_start(out=gain[:], in_=norm_w.rearrange("(p t) -> p t", t=PACK))
+        nc.sync.dma_start(out=w_raw[:, 0], in_=q_w.rearrange("(r p) h -> p r h", p=P))
+        nc.sync.dma_start(out=w_raw[:, 1], in_=k_w.rearrange("(r p) h -> p r h", p=P))
+        for b in range(1, B):
+            load_hidden(b)
+            if b % MEMORY_LOAD == 1:
+                first = b - 1
+                nc.sync.dma_start(
+                    out=mem_all[:, first : first + MEMORY_LOAD],
+                    in_=memory_state[first : first + MEMORY_LOAD].rearrange("b p h -> p b h"),
+                )
+
+        rms_of = {}
+        rstd_of = {}
+        scaled_of = {}
+        turned_of = {}
+        grouped_of = {}
+        codes_of = {}
+        scales_of = {}
+        acc_of = {}
+        result_of = {}
+
+        def squares(b):
+            sumsq = stats.tile([P, TOKEN_TILES], F32)
+            for j in range(TOKEN_TILES):
+                unused = squares_pool.tile([P, H], BF16)
+                nc.scalar.activation(
+                    out=unused[:], in_=x_all[:, b, j, :], func=ACT.Square,
+                    accum_out=sumsq[:, j : j + 1],
+                )
+            rms_of[b] = stats.tile([P, TOKEN_TILES], F32, name="rms")
+            nc.scalar.activation(
+                out=rms_of[b][:], in_=sumsq[:], func=ACT.Sqrt, bias=eps[:, 0:1], scale=1.0 / H
+            )
+
+        def reciprocal(b):
+            rstd_of[b] = stats.tile([P, TOKEN_TILES], F32, name="rstd")
+            nc.vector.reciprocal(out=rstd_of[b][:], in_=rms_of[b][:])
+
+        def scale(b):
+            for j in range(TOKEN_TILES):
+                scaled = scaled_pool.tile([P, PACK, P], F32, name="scaled")
+                scaled_of[b, j] = scaled
+                nc.gpsimd.tensor_scalar(
+                    out=scaled[:],
+                    in0=x_all[:, b, j, :].rearrange("p (i t) -> p t i", t=PACK),
+                    scalar1=rstd_of[b][:, j : j + 1],
+                    scalar2=1.0,
+                    op0=ALU.mult,
+                    op1=ALU.mult,
+                )
+
+        def turn(b):
+            for j in range(TOKEN_TILES):
+                turned = turned_psum.tile([P, PACK, P], F32, name="turned")
+                turned_of[b, j] = turned
+                for t in range(PACK):
+                    nc.tensor.transpose(turned[:, t, :], scaled_of[b, j][:, t, :], ident[:])
+            turned = turned_psum.tile([P, 2, P], F32, name="turned")
+            turned_of[b, TOKEN_TILES] = turned
+            for u in range(2):
+                nc.tensor.transpose(
+                    turned[:, u, :], mem_all[:, b, :].bitcast(F32)[:, u : 2 * P : 2], ident[:]
+                )
+
+        def leave(b, scalar_is_free):
+            grouped = grouped_pool.tile([P, POOL_TILES, P, PACK], BF16, align_bytes=64, name="grouped")
+            grouped_of[b] = grouped
+            for j in range(TOKEN_TILES):
+                nc.vector.tensor_tensor(
+                    out=grouped[:, j],
+                    in0=turned_of[b, j][:].rearrange("p t k -> p k t"),
+                    in1=gain[:].unsqueeze(1).to_broadcast([P, P, PACK]),
+                    op=ALU.mult,
+                )
+            words = (
+                grouped[:, TOKEN_TILES].rearrange("p k t -> p (k t)").bitcast(F32)
+                .rearrange("p (k u) -> p k u", u=2)
+            )
+            source = turned_of[b, TOKEN_TILES][:].rearrange("p u k -> p k u")
+            if scalar_is_free:
+                nc.scalar.copy(out=words, in_=source)
+            else:
+                nc.vector.tensor_copy(out=words, in_=source)
+
+        def quantise(b):
+            codes_of[b] = mx_pool.tile([P, POOL_TILES * P], U32, align_bytes=64, name="codes")
+            scales_of[b] = mx_pool.tile([P, POOL_TILES * P], U8, align_bytes=64, name="scales")
+            nc.vector.quantize_mx(
+                out=codes_of[b][:].bitcast(FP8X4),
+                scales=scales_of[b][:],
+                in_=grouped_of[b][:].rearrange("p j k t -> p (j k t)"),
+            )
+
+        def multiply(b):
+            for j in range(POOL_TILES):
+                first = 0 if j < TOKEN_TILES else D
+                cols = slice(j * P, (j + 1) * P)
+                acc_of[b, j] = acc_psum.tile([P, 2 * D - first], F32, name="acc")
+                nc.tensor.matmul_mx(
+                    out=acc_of[b, j][:],
+                    lhsT=codes_of[b][:, cols].bitcast(FP8X4),
+                    lhsT_scale=scales_of[b][:, cols],
+                    rhs=w_codes[:, first : 2 * D].bitcast(FP8X4),
+                    rhs_scale=w_scales[:, first : 2 * D],
+                    start=True,
+                    stop=True,
+                )
+
+        def copy_out(b, scalar_is_free):
+            qk = result_pool.tile([P, 2, TOKEN_TILES, D], F32, name="qk")
+            k_mem = result_pool.tile([P, D], F32, name="k_mem")
+            result_of[b] = (qk, k_mem)
+            for j in range(TOKEN_TILES):
+                source = acc_of[b, j][:].rearrange("p (m d) -> p m d", m=2)
+                if j < TOKEN_TILES - 1 or scalar_is_free:
+                    nc.scalar.copy(out=qk[:, :, j, :], in_=source)
+                else:
+                    nc.vector.tensor_copy(out=qk[:, :, j, :], in_=source)
+            nc.scalar.copy(out=k_mem[:], in_=acc_of[b, TOKEN_TILES][:])
+
+        def store(b):
+            qk, k_mem = result_of[b]
+            nc.sync.dma_start(
+                out=out_0[b].rearrange("(p j) d -> p j d", j=TOKEN_TILES), in_=qk[:, 0]
+            )
+            nc.sync.dma_start(
+                out=out_1[b, 0:S, :].rearrange("(p j) d -> p j d", j=TOKEN_TILES), in_=qk[:, 1]
+            )
+            nc.sync.dma_start(out=out_1[b, S : S + P, :], in_=k_mem[:])
+
+        w_grouped = keep.tile([P, 2 * D, PACK], BF16, align_bytes=64)
+        w_codes = keep.tile([P, 2 * D], U32, align_bytes=64)
+        w_scales = keep.tile([P, 2 * D], U8, align_bytes=64)
+
+        def prepare_weights():
+            w_words = w_grouped[:].rearrange("p c t -> p (c t)").bitcast(F32)
+            for m in range(2):
+                w_turned = turned_psum.tile([P, 2, D], F32, name="turned")
+                for r in range(2):
+                    for u in range(2):
+                        nc.tensor.transpose(
+                            w_turned[:, u, r * P : (r + 1) * P],
+                            w_raw[:, m, r, :].bitcast(F32)[:, u : 2 * P : 2],
+                            ident[:],
+                        )
+                nc.vector.tensor_copy(
+                    out=w_words[:, m * 2 * D : (m + 1) * 2 * D].rearrange("p (c u) -> p c u", u=2),
+                    in_=w_turned[:].rearrange("p u c -> p c u"),
+                )
+            nc.vector.quantize_mx(
+                out=w_codes[:].bitcast(FP8X4),
+                scales=w_scales[:],
+                in_=w_grouped[:].rearrange("p c t -> p (c t)"),
+            )
+
+        squares(0)
+        reciprocal(0)
+        prepare_weights()
+        for step in range(1 - SQUARES_AHEAD, B):
+            scalar_is_free = step + SQUARES_AHEAD >= B
+            if step + SQUARES_AHEAD < B:
+                squares(step + SQUARES_AHEAD)
+            if 0 <= step + SCALE_AHEAD < B:
+                scale(step + SCALE_AHEAD)
+            if 0 <= step + TURN_AHEAD < B:
+                turn(step + TURN_AHEAD)
+                leave(step + TURN_AHEAD, scalar_is_free)
+            if step >= 0:
+                multiply(step)
+                copy_out(step, scalar_is_free)
+            if 0 <= step + TURN_AHEAD < B:
+                quantise(step + TURN_AHEAD)
+            if step + SQUARES_AHEAD < B:
+                reciprocal(step + SQUARES_AHEAD)
+            if step >= 0:
+                store(step)

@@ -18,13 +18,16 @@ S = 384
 H = 512
 D = 256
 EPS = 1e-6
-TOKEN_TILES = S // P
-POOL_TILES = TOKEN_TILES + 1
-MEMORY_LOAD = 4
-
+TILES = S // P
+HEAD = 0
 FLOPS = 2 * B * (S + S + P) * D * H
-
-SQUARES_AHEAD = 3
+KEEP_BUSY = 64
+SQUARES_AHEAD = 4
+PRE = (6, 2)
+FINE = 3
+VSQ = [(0, 2)]
+EARLY = 2
+EB = 128
 SCALE_AHEAD = 2
 TURN_AHEAD = 1
 
@@ -35,14 +38,14 @@ def tile_memresprojections_pa_t_kernel(
     nc = tc.nc
     with ExitStack() as ctx:
         keep = ctx.enter_context(tc.tile_pool(name="keep", bufs=1))
-        stats = ctx.enter_context(tc.tile_pool(name="stats", bufs=4))
+        stats = ctx.enter_context(tc.tile_pool(name="stats", bufs=8))
         squares_pool = ctx.enter_context(tc.tile_pool(name="squares", bufs=4))
-        scaled_pool = ctx.enter_context(tc.tile_pool(name="scaled", bufs=2 * TOKEN_TILES))
-        grouped_pool = ctx.enter_context(tc.tile_pool(name="grouped", bufs=2))
-        mx_pool = ctx.enter_context(tc.tile_pool(name="mx", bufs=3))
-        result_pool = ctx.enter_context(tc.tile_pool(name="result", bufs=5))
-        turned_psum = ctx.enter_context(tc.psum_pool(name="turned", bufs=POOL_TILES))
-        acc_psum = ctx.enter_context(tc.psum_pool(name="acc", bufs=POOL_TILES))
+        scaled_pool = ctx.enter_context(tc.tile_pool(name="scaled", bufs=12))
+        grouped_pool = ctx.enter_context(tc.tile_pool(name="grouped", bufs=3))
+        mx_pool = ctx.enter_context(tc.tile_pool(name="mx", bufs=4))
+        result_pool = ctx.enter_context(tc.tile_pool(name="result", bufs=6))
+        turned_psum = ctx.enter_context(tc.psum_pool(name="turned", bufs=4))
+        acc_psum = ctx.enter_context(tc.psum_pool(name="acc", bufs=4))
         ctx.enter_context(tc.manual_schedule())
 
         eps = keep.tile([P, 1], F32)
@@ -52,58 +55,83 @@ def tile_memresprojections_pa_t_kernel(
         ident = keep.tile([P, P], F32)
         make_identity(nc, ident[:])
 
-        x_all = keep.tile([P, B, TOKEN_TILES, H], BF16)
+        x_all = keep.tile([P, B, TILES, H], BF16)
         mem_all = keep.tile([P, B, H], BF16)
         w_raw = keep.tile([P, 2, 2, H], BF16)
         gain = keep.tile([P, PACK], BF16)
 
         def load_hidden(b):
             nc.sync.dma_start(
-                out=x_all[:, b], in_=hidden_states[b].rearrange("(p j) h -> p j h", j=TOKEN_TILES)
+                out=x_all[:, b], in_=hidden_states[b].rearrange("(p j) h -> p j h", j=TILES)
             )
 
-        load_hidden(0)
-        nc.sync.dma_start(out=gain[:], in_=norm_w.rearrange("(p t) -> p t", t=PACK))
+        def load_memory(first, count):
+            nc.sync.dma_start(
+                out=mem_all[:, first : first + count],
+                in_=memory_state[first : first + count].rearrange("b p h -> p b h"),
+            )
+
+        def load_tile(b, j):
+            nc.sync.dma_start(
+                out=x_all[:, b, j], in_=hidden_states[b].rearrange("(p j) h -> p j h", j=TILES)[:, j]
+            )
+
+        for j in range(TILES):
+            load_tile(0, j)
         nc.sync.dma_start(out=w_raw[:, 0], in_=q_w.rearrange("(r p) h -> p r h", p=P))
         nc.sync.dma_start(out=w_raw[:, 1], in_=k_w.rearrange("(r p) h -> p r h", p=P))
-        for b in range(1, B):
+        load_hidden(1)
+        nc.sync.dma_start(out=gain[:], in_=norm_w.rearrange("(p t) -> p t", t=PACK))
+        load_memory(0, 2)
+        load_hidden(2)
+        load_memory(2, 2)
+        for b in range(3, B):
             load_hidden(b)
-            if b % MEMORY_LOAD == 1:
-                first = b - 1
-                nc.sync.dma_start(
-                    out=mem_all[:, first : first + MEMORY_LOAD],
-                    in_=memory_state[first : first + MEMORY_LOAD].rearrange("b p h -> p b h"),
-                )
+            if b % 4 == 3 and b + 1 < B:
+                load_memory(b + 1, 4)
 
+        sumsq_of = {}
         rms_of = {}
         rstd_of = {}
         scaled_of = {}
         turned_of = {}
         grouped_of = {}
         codes_of = {}
-        scales_of = {}
         acc_of = {}
-        result_of = {}
+        qk_of = {}
+        k_of = {}
+
+        def has_memory(b):
+            return True
 
         def squares(b):
-            sumsq = stats.tile([P, TOKEN_TILES], F32)
-            for j in range(TOKEN_TILES):
-                unused = squares_pool.tile([P, H], BF16)
+            sumsq_of[b] = stats.tile([P, TILES], F32, name="sumsq")
+            for j in range(TILES):
+                if (b, j) in VSQ:
+                    junk = keep.tile([P, H], F32, name="junk")
+                    nc.vector.scalar_tensor_tensor(
+                        out=junk[:], in0=x_all[:, b, j, :], scalar=1.0, in1=x_all[:, b, j, :],
+                        op0=ALU.mult, op1=ALU.mult, accum_out=sumsq_of[b][:, j : j + 1],
+                    )
+                    continue
+                unused = squares_pool.tile([P, H], BF16, name="unused")
                 nc.scalar.activation(
                     out=unused[:], in_=x_all[:, b, j, :], func=ACT.Square,
-                    accum_out=sumsq[:, j : j + 1],
+                    accum_out=sumsq_of[b][:, j : j + 1],
                 )
-            rms_of[b] = stats.tile([P, TOKEN_TILES], F32, name="rms")
+
+        def root(b):
+            rms_of[b] = stats.tile([P, TILES], F32, name="rms")
             nc.scalar.activation(
-                out=rms_of[b][:], in_=sumsq[:], func=ACT.Sqrt, bias=eps[:, 0:1], scale=1.0 / H
+                out=rms_of[b][:], in_=sumsq_of[b][:], func=ACT.Sqrt, bias=eps[:, 0:1], scale=1.0 / H
             )
 
         def reciprocal(b):
-            rstd_of[b] = stats.tile([P, TOKEN_TILES], F32, name="rstd")
+            rstd_of[b] = stats.tile([P, TILES], F32, name="rstd")
             nc.vector.reciprocal(out=rstd_of[b][:], in_=rms_of[b][:])
 
         def scale(b):
-            for j in range(TOKEN_TILES):
+            for j in range(TILES):
                 scaled = scaled_pool.tile([P, PACK, P], F32, name="scaled")
                 scaled_of[b, j] = scaled
                 nc.gpsimd.tensor_scalar(
@@ -115,93 +143,151 @@ def tile_memresprojections_pa_t_kernel(
                     op1=ALU.mult,
                 )
 
+        def words_of(m):
+            return [mem_all[:, m, :].bitcast(F32)[:, u : 2 * P : 2] for u in range(2)]
+
         def turn(b):
-            for j in range(TOKEN_TILES):
+            if has_memory(b):
+                turned = turned_psum.tile([P, 2, P], F32, name="turned")
+                turned_of[b, TILES] = turned
+                for u in range(2):
+                    nc.tensor.transpose(turned[:, u, :], words_of(b + HEAD)[u], ident[:])
+            for j in range(TILES):
                 turned = turned_psum.tile([P, PACK, P], F32, name="turned")
                 turned_of[b, j] = turned
+                w = EB if b < EARLY else KEEP_BUSY
+                if w:
+                    nc.tensor.matmul(
+                        turned[:].rearrange("p t k -> p (t k)")[:, :w],
+                        lhsT=ident[:], rhs=ident[:, :w], start=True, stop=True,
+                    )
                 for t in range(PACK):
                     nc.tensor.transpose(turned[:, t, :], scaled_of[b, j][:, t, :], ident[:])
-            turned = turned_psum.tile([P, 2, P], F32, name="turned")
-            turned_of[b, TOKEN_TILES] = turned
-            for u in range(2):
-                nc.tensor.transpose(
-                    turned[:, u, :], mem_all[:, b, :].bitcast(F32)[:, u : 2 * P : 2], ident[:]
-                )
 
         def leave(b, scalar_is_free):
-            grouped = grouped_pool.tile([P, POOL_TILES, P, PACK], BF16, align_bytes=64, name="grouped")
+            grouped = grouped_pool.tile([P, 4, P, PACK], BF16, align_bytes=64, name="grouped")
             grouped_of[b] = grouped
-            for j in range(TOKEN_TILES):
+            codes = mx_pool.tile([P, 4 * P], U32, align_bytes=64, name="codes")
+            scales = mx_pool.tile([P, 4 * P], U8, align_bytes=64, name="scales")
+            codes_of[b] = (codes, scales)
+            if has_memory(b):
+                words = (
+                    grouped[:, TILES].rearrange("p k t -> p (k t)").bitcast(F32)
+                    .rearrange("p (k u) -> p k u", u=2)
+                )
+                source = turned_of[b, TILES][:].rearrange("p u k -> p k u")
+                if scalar_is_free:
+                    nc.scalar.copy(out=words, in_=source)
+                else:
+                    nc.vector.tensor_copy(out=words, in_=source)
+            for j in range(TILES):
                 nc.vector.tensor_tensor(
                     out=grouped[:, j],
                     in0=turned_of[b, j][:].rearrange("p t k -> p k t"),
                     in1=gain[:].unsqueeze(1).to_broadcast([P, P, PACK]),
                     op=ALU.mult,
                 )
-            words = (
-                grouped[:, TOKEN_TILES].rearrange("p k t -> p (k t)").bitcast(F32)
-                .rearrange("p (k u) -> p k u", u=2)
+                if b == B - 1 and j == 1:
+                    quantise_tiles(b, 0, 2)
+
+        def quantise_tiles(b, first, last):
+            codes, scales = codes_of[b]
+            nc.vector.quantize_mx(
+                out=codes[:, first * P : last * P].bitcast(FP8X4),
+                scales=scales[:, first * P : last * P],
+                in_=grouped_of[b][:, first:last].rearrange("p j k t -> p (j k t)"),
             )
-            source = turned_of[b, TOKEN_TILES][:].rearrange("p u k -> p k u")
-            if scalar_is_free:
-                nc.scalar.copy(out=words, in_=source)
-            else:
-                nc.vector.tensor_copy(out=words, in_=source)
 
         def quantise(b):
-            codes_of[b] = mx_pool.tile([P, POOL_TILES * P], U32, align_bytes=64, name="codes")
-            scales_of[b] = mx_pool.tile([P, POOL_TILES * P], U8, align_bytes=64, name="scales")
-            nc.vector.quantize_mx(
-                out=codes_of[b][:].bitcast(FP8X4),
-                scales=scales_of[b][:],
-                in_=grouped_of[b][:].rearrange("p j k t -> p (j k t)"),
+            if b < B - 1:
+                quantise_tiles(b, 0, 4)
+            else:
+                quantise_tiles(b, 2, 4)
+
+        def product(acc, codes, j, first):
+            nc.tensor.matmul_mx(
+                out=acc,
+                lhsT=codes[0][:, j * P : (j + 1) * P].bitcast(FP8X4),
+                lhsT_scale=codes[1][:, j * P : (j + 1) * P],
+                rhs=w_codes[:, first : 2 * D].bitcast(FP8X4),
+                rhs_scale=w_scales[:, first : 2 * D],
+                start=True,
+                stop=True,
             )
 
         def multiply(b):
-            for j in range(POOL_TILES):
-                first = 0 if j < TOKEN_TILES else D
-                cols = slice(j * P, (j + 1) * P)
-                acc_of[b, j] = acc_psum.tile([P, 2 * D - first], F32, name="acc")
-                nc.tensor.matmul_mx(
-                    out=acc_of[b, j][:],
-                    lhsT=codes_of[b][:, cols].bitcast(FP8X4),
-                    lhsT_scale=scales_of[b][:, cols],
-                    rhs=w_codes[:, first : 2 * D].bitcast(FP8X4),
-                    rhs_scale=w_scales[:, first : 2 * D],
-                    start=True,
-                    stop=True,
-                )
+            for j in range(TILES):
+                acc_of[b, j] = acc_psum.tile([P, 2 * D], F32, name="acc")
+                product(acc_of[b, j][:], codes_of[b], j, 0)
+            if has_memory(b):
+                acc_of[b, TILES] = acc_psum.tile([P, D], F32, name="acc")
+                product(acc_of[b, TILES][:], codes_of[b], TILES, D)
+
+        def on_vector(b, j, scalar_is_free):
+            return j == 2
+
+        def move(on_v, out, in_):
+            if on_v:
+                nc.vector.tensor_copy(out=out, in_=in_)
+            else:
+                nc.scalar.copy(out=out, in_=in_)
 
         def copy_out(b, scalar_is_free):
-            qk = result_pool.tile([P, 2, TOKEN_TILES, D], F32, name="qk")
-            k_mem = result_pool.tile([P, D], F32, name="k_mem")
-            result_of[b] = (qk, k_mem)
-            for j in range(TOKEN_TILES):
+            qk = result_pool.tile([P, 2, TILES, D], F32, name="qk")
+            qk_of[b] = qk
+            for j in range(TILES):
                 source = acc_of[b, j][:].rearrange("p (m d) -> p m d", m=2)
-                if j < TOKEN_TILES - 1 or scalar_is_free:
-                    nc.scalar.copy(out=qk[:, :, j, :], in_=source)
-                else:
-                    nc.vector.tensor_copy(out=qk[:, :, j, :], in_=source)
-            nc.scalar.copy(out=k_mem[:], in_=acc_of[b, TOKEN_TILES][:])
+                if b == B - 1:
+                    move(False, qk[:, 0, j, :], source[:, 0, :])
+                    move(True, qk[:, 1, j, :], source[:, 1, :])
+                    store_tile(b, j)
+                    continue
+                move(on_vector(b, j, scalar_is_free), qk[:, :, j, :], source)
+                if b >= B - FINE:
+                    store_tile(b, j)
+                if j == 0 and b + SQUARES_AHEAD < B:
+                    root(b + SQUARES_AHEAD)
+            k_of[b] = result_pool.tile([P, D], F32, name="k_mem")
+            move(False, k_of[b][:], acc_of[b, TILES][:])
+            if b >= B - FINE:
+                nc.sync.dma_start(out=out_1[b + HEAD, S : S + P, :], in_=k_of[b][:])
+
+        def store_tile(b, j):
+            nc.sync.dma_start(
+                out=out_0[b].rearrange("(p j) d -> p j d", j=TILES)[:, j, :], in_=qk_of[b][:, 0, j]
+            )
+            nc.sync.dma_start(
+                out=out_1[b, 0:S, :].rearrange("(p j) d -> p j d", j=TILES)[:, j, :],
+                in_=qk_of[b][:, 1, j],
+            )
 
         def store(b):
-            qk, k_mem = result_of[b]
+            if b >= B - FINE:
+                return
             nc.sync.dma_start(
-                out=out_0[b].rearrange("(p j) d -> p j d", j=TOKEN_TILES), in_=qk[:, 0]
+                out=out_0[b].rearrange("(p j) d -> p j d", j=TILES), in_=qk_of[b][:, 0]
             )
             nc.sync.dma_start(
-                out=out_1[b, 0:S, :].rearrange("(p j) d -> p j d", j=TOKEN_TILES), in_=qk[:, 1]
+                out=out_1[b, 0:S, :].rearrange("(p j) d -> p j d", j=TILES), in_=qk_of[b][:, 1]
             )
-            nc.sync.dma_start(out=out_1[b, S : S + P, :], in_=k_mem[:])
+            if has_memory(b):
+                nc.sync.dma_start(out=out_1[b + HEAD, S : S + P, :], in_=k_of[b][:])
 
         w_grouped = keep.tile([P, 2 * D, PACK], BF16, align_bytes=64)
         w_codes = keep.tile([P, 2 * D], U32, align_bytes=64)
         w_scales = keep.tile([P, 2 * D], U8, align_bytes=64)
 
-        def prepare_weights():
+        def keep_busy(bank, columns, times):
+            for i in range(times):
+                nc.tensor.matmul(
+                    bank[:, :columns], lhsT=ident[:], rhs=ident[:, :columns], start=True, stop=True
+                )
+
+        def weights_in():
             w_words = w_grouped[:].rearrange("p c t -> p (c t)").bitcast(F32)
             for m in range(2):
                 w_turned = turned_psum.tile([P, 2, D], F32, name="turned")
+                keep_busy(w_turned[:].rearrange("p u c -> p (u c)"), P, PRE[m])
                 for r in range(2):
                     for u in range(2):
                         nc.tensor.transpose(
@@ -213,6 +299,8 @@ def tile_memresprojections_pa_t_kernel(
                     out=w_words[:, m * 2 * D : (m + 1) * 2 * D].rearrange("p (c u) -> p c u", u=2),
                     in_=w_turned[:].rearrange("p u c -> p c u"),
                 )
+
+        def weights_quantise():
             nc.vector.quantize_mx(
                 out=w_codes[:].bitcast(FP8X4),
                 scales=w_scales[:],
@@ -220,14 +308,22 @@ def tile_memresprojections_pa_t_kernel(
             )
 
         squares(0)
+        root(0)
         reciprocal(0)
-        prepare_weights()
+        scale(0)
+        weights_in()
+        weights_quantise()
         for step in range(1 - SQUARES_AHEAD, B):
             scalar_is_free = step + SQUARES_AHEAD >= B
             if step + SQUARES_AHEAD < B:
                 squares(step + SQUARES_AHEAD)
-            if 0 <= step + SCALE_AHEAD < B:
-                scale(step + SCALE_AHEAD)
+                if step < 0:
+                    root(step + SQUARES_AHEAD)
+                if step + SQUARES_AHEAD == 1:
+                    reciprocal(1)
+                    scale(1)
+            if 1 < step + 2 < B:
+                scale(step + 2)
             if 0 <= step + TURN_AHEAD < B:
                 turn(step + TURN_AHEAD)
                 leave(step + TURN_AHEAD, scalar_is_free)
@@ -236,7 +332,7 @@ def tile_memresprojections_pa_t_kernel(
                 copy_out(step, scalar_is_free)
             if 0 <= step + TURN_AHEAD < B:
                 quantise(step + TURN_AHEAD)
-            if step + SQUARES_AHEAD < B:
-                reciprocal(step + SQUARES_AHEAD)
+            if 1 < step + 3 < B:
+                reciprocal(step + 3)
             if step >= 0:
                 store(step)

@@ -23,11 +23,25 @@ HEAD = 0
 FLOPS = 2 * B * (S + S + P) * D * H
 KEEP_BUSY = 64
 SQUARES_AHEAD = 4
-PRE = (6, 2)
+PRE = (4, 1)
 FINE = 3
 VSQ = [(0, 2)]
 EARLY = 2
 EB = 128
+VC = ()
+BMOD = 2
+BSET = ()
+VCT = ()
+VM = (0, 1)
+VCB = None
+WQ_FIRST = False
+ARS = True
+RB = 0
+LO = 0
+SPLIT0 = True
+SB = 12
+BX = (0, 1)
+BXT = False
 SCALE_AHEAD = 2
 TURN_AHEAD = 1
 
@@ -40,7 +54,8 @@ def tile_memresprojections_pa_t_kernel(
         keep = ctx.enter_context(tc.tile_pool(name="keep", bufs=1))
         stats = ctx.enter_context(tc.tile_pool(name="stats", bufs=8))
         squares_pool = ctx.enter_context(tc.tile_pool(name="squares", bufs=4))
-        scaled_pool = ctx.enter_context(tc.tile_pool(name="scaled", bufs=12))
+        normed_pool = ctx.enter_context(tc.tile_pool(name="normed", bufs=4))
+        scaled_pool = ctx.enter_context(tc.tile_pool(name="scaled", bufs=SB))
         grouped_pool = ctx.enter_context(tc.tile_pool(name="grouped", bufs=3))
         mx_pool = ctx.enter_context(tc.tile_pool(name="mx", bufs=4))
         result_pool = ctx.enter_context(tc.tile_pool(name="result", bufs=6))
@@ -51,7 +66,7 @@ def tile_memresprojections_pa_t_kernel(
         eps = keep.tile([P, 1], F32)
         nc.vector.memset(eps[:], EPS)
         warm = keep.tile([P, 1], F32)
-        nc.scalar.activation(out=warm[:], in_=eps[:], func=ACT.Sqrt)
+        nc.scalar.activation(out=warm[:], in_=eps[:], func=ACT.Abs_reciprocal_sqrt)
         ident = keep.tile([P, P], F32)
         make_identity(nc, ident[:])
 
@@ -78,10 +93,14 @@ def tile_memresprojections_pa_t_kernel(
 
         for j in range(TILES):
             load_tile(0, j)
+            if j == 0:
+                nc.sync.dma_start(out=gain[:], in_=norm_w.rearrange("(p t) -> p t", t=PACK))
+        if LO == 1:
+            load_hidden(1)
         nc.sync.dma_start(out=w_raw[:, 0], in_=q_w.rearrange("(r p) h -> p r h", p=P))
         nc.sync.dma_start(out=w_raw[:, 1], in_=k_w.rearrange("(r p) h -> p r h", p=P))
-        load_hidden(1)
-        nc.sync.dma_start(out=gain[:], in_=norm_w.rearrange("(p t) -> p t", t=PACK))
+        if LO == 0:
+            load_hidden(1)
         load_memory(0, 2)
         load_hidden(2)
         load_memory(2, 2)
@@ -91,6 +110,7 @@ def tile_memresprojections_pa_t_kernel(
                 load_memory(b + 1, 4)
 
         sumsq_of = {}
+        normed_of = {}
         rms_of = {}
         rstd_of = {}
         scaled_of = {}
@@ -121,17 +141,29 @@ def tile_memresprojections_pa_t_kernel(
                 )
 
         def root(b):
+            if ARS:
+                rstd_of[b] = stats.tile([P, TILES], F32, name="rstd")
+                for lo, hi in ([(0, 2), (2, 3)] if b == 0 and SPLIT0 else [(0, 3)]):
+                    nc.scalar.activation(
+                        out=rstd_of[b][:, lo:hi], in_=sumsq_of[b][:, lo:hi], func=ACT.Abs_reciprocal_sqrt, bias=eps[:, 0:1], scale=1.0 / H
+                    )
+                return
             rms_of[b] = stats.tile([P, TILES], F32, name="rms")
             nc.scalar.activation(
                 out=rms_of[b][:], in_=sumsq_of[b][:], func=ACT.Sqrt, bias=eps[:, 0:1], scale=1.0 / H
             )
 
         def reciprocal(b):
+            if ARS:
+                return
             rstd_of[b] = stats.tile([P, TILES], F32, name="rstd")
             nc.vector.reciprocal(out=rstd_of[b][:], in_=rms_of[b][:])
 
+        def direct(b):
+            return b % BMOD in BSET
+
         def scale(b):
-            for j in range(TILES):
+            for j in range(TILES - 1 if direct(b) else TILES):
                 scaled = scaled_pool.tile([P, PACK, P], F32, name="scaled")
                 scaled_of[b, j] = scaled
                 nc.gpsimd.tensor_scalar(
@@ -147,12 +179,7 @@ def tile_memresprojections_pa_t_kernel(
             return [mem_all[:, m, :].bitcast(F32)[:, u : 2 * P : 2] for u in range(2)]
 
         def turn(b):
-            if has_memory(b):
-                turned = turned_psum.tile([P, 2, P], F32, name="turned")
-                turned_of[b, TILES] = turned
-                for u in range(2):
-                    nc.tensor.transpose(turned[:, u, :], words_of(b + HEAD)[u], ident[:])
-            for j in range(TILES):
+            for j in range(TILES - 1 if direct(b) else TILES):
                 turned = turned_psum.tile([P, PACK, P], F32, name="turned")
                 turned_of[b, j] = turned
                 w = EB if b < EARLY else KEEP_BUSY
@@ -163,6 +190,20 @@ def tile_memresprojections_pa_t_kernel(
                     )
                 for t in range(PACK):
                     nc.tensor.transpose(turned[:, t, :], scaled_of[b, j][:, t, :], ident[:])
+            turned = turned_psum.tile([P, 2, 2, P], F32, name="turned")
+            turned_of[b, "words"] = turned
+            w = EB if b < EARLY else KEEP_BUSY
+            if w and direct(b):
+                nc.tensor.matmul(
+                    turned[:].rearrange("p r u k -> p (r u k)")[:, :w],
+                    lhsT=ident[:], rhs=ident[:, :w], start=True, stop=True,
+                )
+            sources = (mem_all[:, b, :], normed_of[b][:]) if direct(b) else (mem_all[:, b, :],)
+            for r, source in enumerate(sources):
+                for u in range(2):
+                    nc.tensor.transpose(
+                        turned[:, 1 - r, u, :], source.bitcast(F32)[:, u : 2 * P : 2], ident[:]
+                    )
 
         def leave(b, scalar_is_free):
             grouped = grouped_pool.tile([P, 4, P, PACK], BF16, align_bytes=64, name="grouped")
@@ -170,17 +211,7 @@ def tile_memresprojections_pa_t_kernel(
             codes = mx_pool.tile([P, 4 * P], U32, align_bytes=64, name="codes")
             scales = mx_pool.tile([P, 4 * P], U8, align_bytes=64, name="scales")
             codes_of[b] = (codes, scales)
-            if has_memory(b):
-                words = (
-                    grouped[:, TILES].rearrange("p k t -> p (k t)").bitcast(F32)
-                    .rearrange("p (k u) -> p k u", u=2)
-                )
-                source = turned_of[b, TILES][:].rearrange("p u k -> p k u")
-                if scalar_is_free:
-                    nc.scalar.copy(out=words, in_=source)
-                else:
-                    nc.vector.tensor_copy(out=words, in_=source)
-            for j in range(TILES):
+            for j in range(TILES - 1 if direct(b) else TILES):
                 nc.vector.tensor_tensor(
                     out=grouped[:, j],
                     in0=turned_of[b, j][:].rearrange("p t k -> p k t"),
@@ -189,6 +220,13 @@ def tile_memresprojections_pa_t_kernel(
                 )
                 if b == B - 1 and j == 1:
                     quantise_tiles(b, 0, 2)
+            first = 0 if direct(b) else 1
+            move(
+                b % 2 in BX and not scalar_is_free or scalar_is_free and BXT,
+                grouped[:, 2 + first : 4].rearrange("p r k t -> p (r k t)").bitcast(F32)
+                .rearrange("p (r k u) -> p r k u", k=P, u=2),
+                turned_of[b, "words"][:, first:].rearrange("p r u k -> p r k u"),
+            )
 
         def quantise_tiles(b, first, last):
             codes, scales = codes_of[b]
@@ -224,7 +262,9 @@ def tile_memresprojections_pa_t_kernel(
                 product(acc_of[b, TILES][:], codes_of[b], TILES, D)
 
         def on_vector(b, j, scalar_is_free):
-            return j == 2
+            if scalar_is_free:
+                return j in VCT
+            return j in (VC if VCB is None or b % 2 in VCB else ())
 
         def move(on_v, out, in_):
             if on_v:
@@ -248,7 +288,7 @@ def tile_memresprojections_pa_t_kernel(
                 if j == 0 and b + SQUARES_AHEAD < B:
                     root(b + SQUARES_AHEAD)
             k_of[b] = result_pool.tile([P, D], F32, name="k_mem")
-            move(False, k_of[b][:], acc_of[b, TILES][:])
+            move(b % 2 in VM and not scalar_is_free, k_of[b][:], acc_of[b, TILES][:])
             if b >= B - FINE:
                 nc.sync.dma_start(out=out_1[b + HEAD, S : S + P, :], in_=k_of[b][:])
 
@@ -312,27 +352,35 @@ def tile_memresprojections_pa_t_kernel(
         reciprocal(0)
         scale(0)
         weights_in()
-        weights_quantise()
         for step in range(1 - SQUARES_AHEAD, B):
             scalar_is_free = step + SQUARES_AHEAD >= B
             if step + SQUARES_AHEAD < B:
                 squares(step + SQUARES_AHEAD)
                 if step < 0:
                     root(step + SQUARES_AHEAD)
-                if step + SQUARES_AHEAD == 1:
-                    reciprocal(1)
-                    scale(1)
             if 1 < step + 2 < B:
                 scale(step + 2)
             if 0 <= step + TURN_AHEAD < B:
                 turn(step + TURN_AHEAD)
+                if step == -1:
+                    reciprocal(1)
+                    scale(1)
+                if RB == 2 and 1 < step + 3 < B:
+                    reciprocal(step + 3)
                 leave(step + TURN_AHEAD, scalar_is_free)
+                if RB == 1 and 1 < step + 3 < B:
+                    reciprocal(step + 3)
+            if step == -1:
+                if WQ_FIRST:
+                    weights_quantise()
             if step >= 0:
                 multiply(step)
                 copy_out(step, scalar_is_free)
             if 0 <= step + TURN_AHEAD < B:
                 quantise(step + TURN_AHEAD)
-            if 1 < step + 3 < B:
+                if step == -1 and not WQ_FIRST:
+                    weights_quantise()
+            if 1 < step + 3 < B and not RB:
                 reciprocal(step + 3)
             if step >= 0:
                 store(step)

@@ -19,31 +19,21 @@ H = 512
 D = 256
 EPS = 1e-6
 TILES = S // P
-HEAD = 0
+ROW_TILES = TILES + 1
+
 FLOPS = 2 * B * (S + S + P) * D * H
-KEEP_BUSY = 64
+
 SQUARES_AHEAD = 4
-PRE = (4, 1)
-FINE = 3
-VSQ = [(0, 2)]
-EARLY = 2
-EB = 128
-VC = ()
-BMOD = 2
-BSET = ()
-VCT = ()
-VM = (0, 1)
-VCB = None
-WQ_FIRST = False
-ARS = True
-RB = 0
-LO = 0
-SPLIT0 = True
-SB = 12
-BX = (0, 1)
-BXT = False
+RECIPROCAL_AHEAD = 3
 SCALE_AHEAD = 2
-TURN_AHEAD = 1
+LEAVE_AHEAD = 1
+
+BUSY_COLUMNS = 64
+BUSY_COLUMNS_FIRST = 128
+FIRST_BATCHES = 2
+
+FINE_STORES = 3
+SHARED_TAIL = 2
 
 
 def tile_memresprojections_pa_t_kernel(
@@ -54,19 +44,18 @@ def tile_memresprojections_pa_t_kernel(
         keep = ctx.enter_context(tc.tile_pool(name="keep", bufs=1))
         stats = ctx.enter_context(tc.tile_pool(name="stats", bufs=8))
         squares_pool = ctx.enter_context(tc.tile_pool(name="squares", bufs=4))
-        normed_pool = ctx.enter_context(tc.tile_pool(name="normed", bufs=4))
-        scaled_pool = ctx.enter_context(tc.tile_pool(name="scaled", bufs=SB))
+        scaled_pool = ctx.enter_context(tc.tile_pool(name="scaled", bufs=4 * TILES))
         grouped_pool = ctx.enter_context(tc.tile_pool(name="grouped", bufs=3))
         mx_pool = ctx.enter_context(tc.tile_pool(name="mx", bufs=4))
         result_pool = ctx.enter_context(tc.tile_pool(name="result", bufs=6))
-        turned_psum = ctx.enter_context(tc.psum_pool(name="turned", bufs=4))
-        acc_psum = ctx.enter_context(tc.psum_pool(name="acc", bufs=4))
+        turned_psum = ctx.enter_context(tc.psum_pool(name="turned", bufs=ROW_TILES))
+        acc_psum = ctx.enter_context(tc.psum_pool(name="acc", bufs=ROW_TILES))
         ctx.enter_context(tc.manual_schedule())
 
         eps = keep.tile([P, 1], F32)
         nc.vector.memset(eps[:], EPS)
         warm = keep.tile([P, 1], F32)
-        nc.scalar.activation(out=warm[:], in_=eps[:], func=ACT.Abs_reciprocal_sqrt)
+        nc.scalar.activation(out=warm[:], in_=eps[:], func=ACT.Sqrt)
         ident = keep.tile([P, P], F32)
         make_identity(nc, ident[:])
 
@@ -75,10 +64,11 @@ def tile_memresprojections_pa_t_kernel(
         w_raw = keep.tile([P, 2, 2, H], BF16)
         gain = keep.tile([P, PACK], BF16)
 
+        def tokens(dram):
+            return dram.rearrange("(p j) f -> p j f", j=TILES)
+
         def load_hidden(b):
-            nc.sync.dma_start(
-                out=x_all[:, b], in_=hidden_states[b].rearrange("(p j) h -> p j h", j=TILES)
-            )
+            nc.sync.dma_start(out=x_all[:, b], in_=tokens(hidden_states[b]))
 
         def load_memory(first, count):
             nc.sync.dma_start(
@@ -86,21 +76,13 @@ def tile_memresprojections_pa_t_kernel(
                 in_=memory_state[first : first + count].rearrange("b p h -> p b h"),
             )
 
-        def load_tile(b, j):
-            nc.sync.dma_start(
-                out=x_all[:, b, j], in_=hidden_states[b].rearrange("(p j) h -> p j h", j=TILES)[:, j]
-            )
-
         for j in range(TILES):
-            load_tile(0, j)
+            nc.sync.dma_start(out=x_all[:, 0, j], in_=tokens(hidden_states[0])[:, j])
             if j == 0:
                 nc.sync.dma_start(out=gain[:], in_=norm_w.rearrange("(p t) -> p t", t=PACK))
-        if LO == 1:
-            load_hidden(1)
+        load_hidden(1)
         nc.sync.dma_start(out=w_raw[:, 0], in_=q_w.rearrange("(r p) h -> p r h", p=P))
         nc.sync.dma_start(out=w_raw[:, 1], in_=k_w.rearrange("(r p) h -> p r h", p=P))
-        if LO == 0:
-            load_hidden(1)
         load_memory(0, 2)
         load_hidden(2)
         load_memory(2, 2)
@@ -110,108 +92,99 @@ def tile_memresprojections_pa_t_kernel(
                 load_memory(b + 1, 4)
 
         sumsq_of = {}
-        normed_of = {}
         rms_of = {}
         rstd_of = {}
         scaled_of = {}
         turned_of = {}
+        words_of = {}
         grouped_of = {}
         codes_of = {}
+        scales_of = {}
         acc_of = {}
         qk_of = {}
-        k_of = {}
-
-        def has_memory(b):
-            return True
+        k_mem_of = {}
 
         def squares(b):
             sumsq_of[b] = stats.tile([P, TILES], F32, name="sumsq")
             for j in range(TILES):
-                if (b, j) in VSQ:
-                    junk = keep.tile([P, H], F32, name="junk")
+                unused = squares_pool.tile([P, H], F32, name="unused")
+                total = sumsq_of[b][:, j : j + 1]
+                x = x_all[:, b, j, :]
+                if b == 0 and j == TILES - 1:
                     nc.vector.scalar_tensor_tensor(
-                        out=junk[:], in0=x_all[:, b, j, :], scalar=1.0, in1=x_all[:, b, j, :],
-                        op0=ALU.mult, op1=ALU.mult, accum_out=sumsq_of[b][:, j : j + 1],
+                        out=unused[:], in0=x, scalar=1.0, in1=x, op0=ALU.mult, op1=ALU.mult,
+                        accum_out=total,
                     )
-                    continue
-                unused = squares_pool.tile([P, H], BF16, name="unused")
-                nc.scalar.activation(
-                    out=unused[:], in_=x_all[:, b, j, :], func=ACT.Square,
-                    accum_out=sumsq_of[b][:, j : j + 1],
-                )
+                else:
+                    nc.scalar.activation(out=unused[:], in_=x, func=ACT.Square, accum_out=total)
 
         def root(b):
-            if ARS:
-                rstd_of[b] = stats.tile([P, TILES], F32, name="rstd")
-                for lo, hi in ([(0, 2), (2, 3)] if b == 0 and SPLIT0 else [(0, 3)]):
-                    nc.scalar.activation(
-                        out=rstd_of[b][:, lo:hi], in_=sumsq_of[b][:, lo:hi], func=ACT.Abs_reciprocal_sqrt, bias=eps[:, 0:1], scale=1.0 / H
-                    )
-                return
             rms_of[b] = stats.tile([P, TILES], F32, name="rms")
             nc.scalar.activation(
                 out=rms_of[b][:], in_=sumsq_of[b][:], func=ACT.Sqrt, bias=eps[:, 0:1], scale=1.0 / H
             )
 
         def reciprocal(b):
-            if ARS:
-                return
             rstd_of[b] = stats.tile([P, TILES], F32, name="rstd")
             nc.vector.reciprocal(out=rstd_of[b][:], in_=rms_of[b][:])
 
-        def direct(b):
-            return b % BMOD in BSET
-
         def scale(b):
-            for j in range(TILES - 1 if direct(b) else TILES):
+            for j in range(TILES):
                 scaled = scaled_pool.tile([P, PACK, P], F32, name="scaled")
                 scaled_of[b, j] = scaled
-                nc.gpsimd.tensor_scalar(
-                    out=scaled[:],
-                    in0=x_all[:, b, j, :].rearrange("p (i t) -> p t i", t=PACK),
-                    scalar1=rstd_of[b][:, j : j + 1],
-                    scalar2=1.0,
-                    op0=ALU.mult,
-                    op1=ALU.mult,
-                )
+                x = x_all[:, b, j, :].rearrange("p (i t) -> p t i", t=PACK)
+                rstd = rstd_of[b][:, j : j + 1]
+                if b >= B - SHARED_TAIL and j == TILES - 1:
+                    nc.scalar.activation(out=scaled[:], in_=x, func=ACT.Copy, scale=rstd)
+                else:
+                    nc.gpsimd.tensor_scalar(
+                        out=scaled[:], in0=x, scalar1=rstd, scalar2=1.0, op0=ALU.mult, op1=ALU.mult
+                    )
 
-        def words_of(m):
-            return [mem_all[:, m, :].bitcast(F32)[:, u : 2 * P : 2] for u in range(2)]
+        def keep_busy(bank, columns):
+            nc.tensor.matmul(
+                bank[:, :columns], lhsT=ident[:], rhs=ident[:, :columns], start=True, stop=True
+            )
+
+        def word_columns(rows, u):
+            return rows.bitcast(F32)[:, u : 2 * P : 2]
 
         def turn(b):
-            for j in range(TILES - 1 if direct(b) else TILES):
+            for j in range(TILES):
                 turned = turned_psum.tile([P, PACK, P], F32, name="turned")
                 turned_of[b, j] = turned
-                w = EB if b < EARLY else KEEP_BUSY
-                if w:
-                    nc.tensor.matmul(
-                        turned[:].rearrange("p t k -> p (t k)")[:, :w],
-                        lhsT=ident[:], rhs=ident[:, :w], start=True, stop=True,
-                    )
+                keep_busy(
+                    turned[:].rearrange("p t k -> p (t k)"),
+                    BUSY_COLUMNS_FIRST if b < FIRST_BATCHES else BUSY_COLUMNS,
+                )
                 for t in range(PACK):
                     nc.tensor.transpose(turned[:, t, :], scaled_of[b, j][:, t, :], ident[:])
-            turned = turned_psum.tile([P, 2, 2, P], F32, name="turned")
-            turned_of[b, "words"] = turned
-            w = EB if b < EARLY else KEEP_BUSY
-            if w and direct(b):
-                nc.tensor.matmul(
-                    turned[:].rearrange("p r u k -> p (r u k)")[:, :w],
-                    lhsT=ident[:], rhs=ident[:, :w], start=True, stop=True,
+            words_of[b] = turned_psum.tile([P, 2, P], F32, name="turned")
+            for u in range(2):
+                nc.tensor.transpose(
+                    words_of[b][:, u, :], word_columns(mem_all[:, b, :], u), ident[:]
                 )
-            sources = (mem_all[:, b, :], normed_of[b][:]) if direct(b) else (mem_all[:, b, :],)
-            for r, source in enumerate(sources):
-                for u in range(2):
-                    nc.tensor.transpose(
-                        turned[:, 1 - r, u, :], source.bitcast(F32)[:, u : 2 * P : 2], ident[:]
-                    )
+
+        def quantise(b, first, last):
+            columns = slice(first * P, last * P)
+            nc.vector.quantize_mx(
+                out=codes_of[b][:, columns].bitcast(FP8X4),
+                scales=scales_of[b][:, columns],
+                in_=grouped_of[b][:, first:last].rearrange("p j k t -> p (j k t)"),
+            )
+
+        def copy(on_vector, out, in_):
+            if on_vector:
+                nc.vector.tensor_copy(out=out, in_=in_)
+            else:
+                nc.scalar.copy(out=out, in_=in_)
 
         def leave(b, scalar_is_free):
-            grouped = grouped_pool.tile([P, 4, P, PACK], BF16, align_bytes=64, name="grouped")
+            grouped = grouped_pool.tile([P, ROW_TILES, P, PACK], BF16, align_bytes=64, name="grouped")
             grouped_of[b] = grouped
-            codes = mx_pool.tile([P, 4 * P], U32, align_bytes=64, name="codes")
-            scales = mx_pool.tile([P, 4 * P], U8, align_bytes=64, name="scales")
-            codes_of[b] = (codes, scales)
-            for j in range(TILES - 1 if direct(b) else TILES):
+            codes_of[b] = mx_pool.tile([P, ROW_TILES * P], U32, align_bytes=64, name="codes")
+            scales_of[b] = mx_pool.tile([P, ROW_TILES * P], U8, align_bytes=64, name="scales")
+            for j in range(TILES):
                 nc.vector.tensor_tensor(
                     out=grouped[:, j],
                     in0=turned_of[b, j][:].rearrange("p t k -> p k t"),
@@ -219,34 +192,20 @@ def tile_memresprojections_pa_t_kernel(
                     op=ALU.mult,
                 )
                 if b == B - 1 and j == 1:
-                    quantise_tiles(b, 0, 2)
-            first = 0 if direct(b) else 1
-            move(
-                b % 2 in BX and not scalar_is_free or scalar_is_free and BXT,
-                grouped[:, 2 + first : 4].rearrange("p r k t -> p (r k t)").bitcast(F32)
-                .rearrange("p (r k u) -> p r k u", k=P, u=2),
-                turned_of[b, "words"][:, first:].rearrange("p r u k -> p r k u"),
+                    quantise(b, 0, 2)
+            copy(
+                not scalar_is_free,
+                out=grouped[:, TILES].rearrange("p k t -> p (k t)").bitcast(F32)
+                .rearrange("p (k u) -> p k u", u=2),
+                in_=words_of[b][:].rearrange("p u k -> p k u"),
             )
 
-        def quantise_tiles(b, first, last):
-            codes, scales = codes_of[b]
-            nc.vector.quantize_mx(
-                out=codes[:, first * P : last * P].bitcast(FP8X4),
-                scales=scales[:, first * P : last * P],
-                in_=grouped_of[b][:, first:last].rearrange("p j k t -> p (j k t)"),
-            )
-
-        def quantise(b):
-            if b < B - 1:
-                quantise_tiles(b, 0, 4)
-            else:
-                quantise_tiles(b, 2, 4)
-
-        def product(acc, codes, j, first):
+        def product(out, b, j, first):
+            rows = slice(j * P, (j + 1) * P)
             nc.tensor.matmul_mx(
-                out=acc,
-                lhsT=codes[0][:, j * P : (j + 1) * P].bitcast(FP8X4),
-                lhsT_scale=codes[1][:, j * P : (j + 1) * P],
+                out=out,
+                lhsT=codes_of[b][:, rows].bitcast(FP8X4),
+                lhsT_scale=scales_of[b][:, rows],
                 rhs=w_codes[:, first : 2 * D].bitcast(FP8X4),
                 rhs_scale=w_scales[:, first : 2 * D],
                 start=True,
@@ -256,91 +215,64 @@ def tile_memresprojections_pa_t_kernel(
         def multiply(b):
             for j in range(TILES):
                 acc_of[b, j] = acc_psum.tile([P, 2 * D], F32, name="acc")
-                product(acc_of[b, j][:], codes_of[b], j, 0)
-            if has_memory(b):
-                acc_of[b, TILES] = acc_psum.tile([P, D], F32, name="acc")
-                product(acc_of[b, TILES][:], codes_of[b], TILES, D)
+                product(acc_of[b, j][:], b, j, 0)
+            acc_of[b, TILES] = acc_psum.tile([P, D], F32, name="acc")
+            product(acc_of[b, TILES][:], b, TILES, D)
 
-        def on_vector(b, j, scalar_is_free):
-            if scalar_is_free:
-                return j in VCT
-            return j in (VC if VCB is None or b % 2 in VCB else ())
+        def store_tile(b, j):
+            nc.sync.dma_start(out=tokens(out_0[b])[:, j, :], in_=qk_of[b][:, 0, j])
+            nc.sync.dma_start(out=tokens(out_1[b, 0:S, :])[:, j, :], in_=qk_of[b][:, 1, j])
 
-        def move(on_v, out, in_):
-            if on_v:
-                nc.vector.tensor_copy(out=out, in_=in_)
-            else:
-                nc.scalar.copy(out=out, in_=in_)
+        def store_memory(b):
+            nc.sync.dma_start(out=out_1[b, S : S + P, :], in_=k_mem_of[b][:])
 
         def copy_out(b, scalar_is_free):
             qk = result_pool.tile([P, 2, TILES, D], F32, name="qk")
             qk_of[b] = qk
+            vector_tile = b >= B - SHARED_TAIL if scalar_is_free else b % 2 == 0
+            vector_memory = not scalar_is_free and b % 2 == 1
             for j in range(TILES):
                 source = acc_of[b, j][:].rearrange("p (m d) -> p m d", m=2)
                 if b == B - 1:
-                    move(False, qk[:, 0, j, :], source[:, 0, :])
-                    move(True, qk[:, 1, j, :], source[:, 1, :])
-                    store_tile(b, j)
-                    continue
-                move(on_vector(b, j, scalar_is_free), qk[:, :, j, :], source)
-                if b >= B - FINE:
+                    copy(False, out=qk[:, 0, j, :], in_=source[:, 0, :])
+                    copy(True, out=qk[:, 1, j, :], in_=source[:, 1, :])
+                else:
+                    copy(vector_tile and j == TILES - 1, out=qk[:, :, j, :], in_=source)
+                if b >= B - FINE_STORES:
                     store_tile(b, j)
                 if j == 0 and b + SQUARES_AHEAD < B:
                     root(b + SQUARES_AHEAD)
-            k_of[b] = result_pool.tile([P, D], F32, name="k_mem")
-            move(b % 2 in VM and not scalar_is_free, k_of[b][:], acc_of[b, TILES][:])
-            if b >= B - FINE:
-                nc.sync.dma_start(out=out_1[b + HEAD, S : S + P, :], in_=k_of[b][:])
-
-        def store_tile(b, j):
-            nc.sync.dma_start(
-                out=out_0[b].rearrange("(p j) d -> p j d", j=TILES)[:, j, :], in_=qk_of[b][:, 0, j]
-            )
-            nc.sync.dma_start(
-                out=out_1[b, 0:S, :].rearrange("(p j) d -> p j d", j=TILES)[:, j, :],
-                in_=qk_of[b][:, 1, j],
-            )
+            k_mem_of[b] = result_pool.tile([P, D], F32, name="k_mem")
+            copy(vector_memory, out=k_mem_of[b][:], in_=acc_of[b, TILES][:])
+            if b >= B - FINE_STORES:
+                store_memory(b)
 
         def store(b):
-            if b >= B - FINE:
-                return
-            nc.sync.dma_start(
-                out=out_0[b].rearrange("(p j) d -> p j d", j=TILES), in_=qk_of[b][:, 0]
-            )
-            nc.sync.dma_start(
-                out=out_1[b, 0:S, :].rearrange("(p j) d -> p j d", j=TILES), in_=qk_of[b][:, 1]
-            )
-            if has_memory(b):
-                nc.sync.dma_start(out=out_1[b + HEAD, S : S + P, :], in_=k_of[b][:])
+            nc.sync.dma_start(out=tokens(out_0[b]), in_=qk_of[b][:, 0])
+            nc.sync.dma_start(out=tokens(out_1[b, 0:S, :]), in_=qk_of[b][:, 1])
+            store_memory(b)
 
         w_grouped = keep.tile([P, 2 * D, PACK], BF16, align_bytes=64)
         w_codes = keep.tile([P, 2 * D], U32, align_bytes=64)
         w_scales = keep.tile([P, 2 * D], U8, align_bytes=64)
 
-        def keep_busy(bank, columns, times):
-            for i in range(times):
-                nc.tensor.matmul(
-                    bank[:, :columns], lhsT=ident[:], rhs=ident[:, :columns], start=True, stop=True
-                )
-
-        def weights_in():
+        def prepare_weights():
             w_words = w_grouped[:].rearrange("p c t -> p (c t)").bitcast(F32)
             for m in range(2):
                 w_turned = turned_psum.tile([P, 2, D], F32, name="turned")
-                keep_busy(w_turned[:].rearrange("p u c -> p (u c)"), P, PRE[m])
+                for repeat in range(4 if m == 0 else 1):
+                    keep_busy(w_turned[:].rearrange("p u c -> p (u c)"), BUSY_COLUMNS_FIRST)
                 for r in range(2):
                     for u in range(2):
                         nc.tensor.transpose(
                             w_turned[:, u, r * P : (r + 1) * P],
-                            w_raw[:, m, r, :].bitcast(F32)[:, u : 2 * P : 2],
+                            word_columns(w_raw[:, m, r, :], u),
                             ident[:],
                         )
                 nc.vector.tensor_copy(
                     out=w_words[:, m * 2 * D : (m + 1) * 2 * D].rearrange("p (c u) -> p c u", u=2),
                     in_=w_turned[:].rearrange("p u c -> p c u"),
                 )
-
-        def weights_quantise():
             nc.vector.quantize_mx(
                 out=w_codes[:].bitcast(FP8X4),
                 scales=w_scales[:],
@@ -351,36 +283,27 @@ def tile_memresprojections_pa_t_kernel(
         root(0)
         reciprocal(0)
         scale(0)
-        weights_in()
+        prepare_weights()
         for step in range(1 - SQUARES_AHEAD, B):
             scalar_is_free = step + SQUARES_AHEAD >= B
-            if step + SQUARES_AHEAD < B:
+            if not scalar_is_free:
                 squares(step + SQUARES_AHEAD)
                 if step < 0:
                     root(step + SQUARES_AHEAD)
-            if 1 < step + 2 < B:
-                scale(step + 2)
-            if 0 <= step + TURN_AHEAD < B:
-                turn(step + TURN_AHEAD)
-                if step == -1:
+            if 2 <= step + SCALE_AHEAD < B:
+                scale(step + SCALE_AHEAD)
+            if 0 <= step + LEAVE_AHEAD < B:
+                turn(step + LEAVE_AHEAD)
+                if step + LEAVE_AHEAD == 0:
                     reciprocal(1)
                     scale(1)
-                if RB == 2 and 1 < step + 3 < B:
-                    reciprocal(step + 3)
-                leave(step + TURN_AHEAD, scalar_is_free)
-                if RB == 1 and 1 < step + 3 < B:
-                    reciprocal(step + 3)
-            if step == -1:
-                if WQ_FIRST:
-                    weights_quantise()
+                leave(step + LEAVE_AHEAD, scalar_is_free)
             if step >= 0:
                 multiply(step)
                 copy_out(step, scalar_is_free)
-            if 0 <= step + TURN_AHEAD < B:
-                quantise(step + TURN_AHEAD)
-                if step == -1 and not WQ_FIRST:
-                    weights_quantise()
-            if 1 < step + 3 < B and not RB:
-                reciprocal(step + 3)
-            if step >= 0:
+            if 2 <= step + RECIPROCAL_AHEAD < B:
+                reciprocal(step + RECIPROCAL_AHEAD)
+            if 0 <= step + LEAVE_AHEAD < B:
+                quantise(step + LEAVE_AHEAD, 0 if step + LEAVE_AHEAD < B - 1 else 2, ROW_TILES)
+            if 0 <= step < B - FINE_STORES:
                 store(step)

@@ -42,12 +42,12 @@ def tile_memresprojections_pa_t_kernel(
     nc = tc.nc
     with ExitStack() as ctx:
         keep = ctx.enter_context(tc.tile_pool(name="keep", bufs=1))
-        stats = ctx.enter_context(tc.tile_pool(name="stats", bufs=8))
+        stats = ctx.enter_context(tc.tile_pool(name="stats", bufs=B))
         squares_pool = ctx.enter_context(tc.tile_pool(name="squares", bufs=4))
-        scaled_pool = ctx.enter_context(tc.tile_pool(name="scaled", bufs=4 * TILES))
+        scaled_pool = ctx.enter_context(tc.tile_pool(name="scaled", bufs=3 * TILES))
         grouped_pool = ctx.enter_context(tc.tile_pool(name="grouped", bufs=3))
         mx_pool = ctx.enter_context(tc.tile_pool(name="mx", bufs=4))
-        result_pool = ctx.enter_context(tc.tile_pool(name="result", bufs=6))
+        result_pool = ctx.enter_context(tc.tile_pool(name="result", bufs=B))
         turned_psum = ctx.enter_context(tc.psum_pool(name="turned", bufs=ROW_TILES))
         acc_psum = ctx.enter_context(tc.psum_pool(name="acc", bufs=ROW_TILES))
         ctx.enter_context(tc.manual_schedule())
@@ -107,7 +107,7 @@ def tile_memresprojections_pa_t_kernel(
         def squares(b):
             sumsq_of[b] = stats.tile([P, TILES], F32, name="sumsq")
             for j in range(TILES):
-                unused = squares_pool.tile([P, H], F32, name="unused")
+                unused = squares_pool.tile([P, H], BF16, name="unused")
                 total = sumsq_of[b][:, j : j + 1]
                 x = x_all[:, b, j, :]
                 if b == 0 and j == TILES - 1:

from contextlib import ExitStack

import concourse.mybir as mybir
from concourse.masks import make_identity

F32 = mybir.dt.float32
BF16 = mybir.dt.bfloat16
U32 = mybir.dt.uint32
U8 = mybir.dt.uint8
FP8X4 = mybir.dt.float8_e4m3fn_x4
ACT = mybir.ActivationFunctionType
ALU = mybir.AluOpType

P = 128
PACK = 4
B = 16
S = 384
H = 512
D = 256
EPS = 1e-6
TILES = S // P
ROW_TILES = TILES + 1

FLOPS = 2 * B * (S + S + P) * D * H

SQUARES_AHEAD = 4
RECIPROCAL_AHEAD = 3
SCALE_AHEAD = 2
LEAVE_AHEAD = 1

BUSY_COLUMNS = 64
BUSY_COLUMNS_FIRST = 128
FIRST_BATCHES = 2

FINE_STORES = 3
SHARED_TAIL = 2


def tile_memresprojections_pa_t_kernel(
    tc, hidden_states, memory_state, q_w, k_w, norm_w, out_0, out_1
):
    nc = tc.nc
    with ExitStack() as ctx:
        keep = ctx.enter_context(tc.tile_pool(name="keep", bufs=1))
        stats = ctx.enter_context(tc.tile_pool(name="stats", bufs=B))
        squares_pool = ctx.enter_context(tc.tile_pool(name="squares", bufs=4))
        scaled_pool = ctx.enter_context(tc.tile_pool(name="scaled", bufs=3 * TILES))
        grouped_pool = ctx.enter_context(tc.tile_pool(name="grouped", bufs=3))
        mx_pool = ctx.enter_context(tc.tile_pool(name="mx", bufs=4))
        result_pool = ctx.enter_context(tc.tile_pool(name="result", bufs=B))
        turned_psum = ctx.enter_context(tc.psum_pool(name="turned", bufs=ROW_TILES))
        acc_psum = ctx.enter_context(tc.psum_pool(name="acc", bufs=ROW_TILES))
        ctx.enter_context(tc.manual_schedule())

        eps = keep.tile([P, 1], F32)
        nc.vector.memset(eps[:], EPS)
        warm = keep.tile([P, 1], F32)
        nc.scalar.activation(out=warm[:], in_=eps[:], func=ACT.Sqrt)
        ident = keep.tile([P, P], F32)
        make_identity(nc, ident[:])

        x_all = keep.tile([P, B, TILES, H], BF16)
        mem_all = keep.tile([P, B, H], BF16)
        w_raw = keep.tile([P, 2, 2, H], BF16)
        gain = keep.tile([P, PACK], BF16)

        def tokens(dram):
            return dram.rearrange("(p j) f -> p j f", j=TILES)

        def load_hidden(b):
            nc.sync.dma_start(out=x_all[:, b], in_=tokens(hidden_states[b]))

        def load_memory(first, count):
            nc.sync.dma_start(
                out=mem_all[:, first : first + count],
                in_=memory_state[first : first + count].rearrange("b p h -> p b h"),
            )

        for j in range(TILES):
            nc.sync.dma_start(out=x_all[:, 0, j], in_=tokens(hidden_states[0])[:, j])
            if j == 0:
                nc.sync.dma_start(out=gain[:], in_=norm_w.rearrange("(p t) -> p t", t=PACK))
        load_hidden(1)
        nc.sync.dma_start(out=w_raw[:, 0], in_=q_w.rearrange("(r p) h -> p r h", p=P))
        nc.sync.dma_start(out=w_raw[:, 1], in_=k_w.rearrange("(r p) h -> p r h", p=P))
        load_memory(0, 2)
        load_hidden(2)
        load_memory(2, 2)
        for b in range(3, B):
            load_hidden(b)
            if b % 4 == 3 and b + 1 < B:
                load_memory(b + 1, 4)

        sumsq_of = {}
        rms_of = {}
        rstd_of = {}
        scaled_of = {}
        turned_of = {}
        words_of = {}
        grouped_of = {}
        codes_of = {}
        scales_of = {}
        acc_of = {}
        qk_of = {}
        k_mem_of = {}

        def squares(b):
            sumsq_of[b] = stats.tile([P, TILES], F32, name="sumsq")
            for j in range(TILES):
                unused = squares_pool.tile([P, H], BF16, name="unused")
                total = sumsq_of[b][:, j : j + 1]
                x = x_all[:, b, j, :]
                if b == 0 and j == TILES - 1:
                    nc.vector.scalar_tensor_tensor(
                        out=unused[:], in0=x, scalar=1.0, in1=x, op0=ALU.mult, op1=ALU.mult,
                        accum_out=total,
                    )
                else:
                    nc.scalar.activation(out=unused[:], in_=x, func=ACT.Square, accum_out=total)

        def root(b):
            rms_of[b] = stats.tile([P, TILES], F32, name="rms")
            nc.scalar.activation(
                out=rms_of[b][:], in_=sumsq_of[b][:], func=ACT.Sqrt, bias=eps[:, 0:1], scale=1.0 / H
            )

        def reciprocal(b):
            rstd_of[b] = stats.tile([P, TILES], F32, name="rstd")
            nc.vector.reciprocal(out=rstd_of[b][:], in_=rms_of[b][:])

        def scale(b):
            for j in range(TILES):
                scaled = scaled_pool.tile([P, PACK, P], F32, name="scaled")
                scaled_of[b, j] = scaled
                x = x_all[:, b, j, :].rearrange("p (i t) -> p t i", t=PACK)
                rstd = rstd_of[b][:, j : j + 1]
                if b >= B - SHARED_TAIL and j == TILES - 1:
                    nc.scalar.activation(out=scaled[:], in_=x, func=ACT.Copy, scale=rstd)
                else:
                    nc.gpsimd.tensor_scalar(
                        out=scaled[:], in0=x, scalar1=rstd, scalar2=1.0, op0=ALU.mult, op1=ALU.mult
                    )

        def keep_busy(bank, columns):
            nc.tensor.matmul(
                bank[:, :columns], lhsT=ident[:], rhs=ident[:, :columns], start=True, stop=True
            )

        def word_columns(rows, u):
            return rows.bitcast(F32)[:, u : 2 * P : 2]

        def turn(b):
            for j in range(TILES):
                turned = turned_psum.tile([P, PACK, P], F32, name="turned")
                turned_of[b, j] = turned
                keep_busy(
                    turned[:].rearrange("p t k -> p (t k)"),
                    BUSY_COLUMNS_FIRST if b < FIRST_BATCHES else BUSY_COLUMNS,
                )
                for t in range(PACK):
                    nc.tensor.transpose(turned[:, t, :], scaled_of[b, j][:, t, :], ident[:])
            words_of[b] = turned_psum.tile([P, 2, P], F32, name="turned")
            for u in range(2):
                nc.tensor.transpose(
                    words_of[b][:, u, :], word_columns(mem_all[:, b, :], u), ident[:]
                )

        def quantise(b, first, last):
            columns = slice(first * P, last * P)
            nc.vector.quantize_mx(
                out=codes_of[b][:, columns].bitcast(FP8X4),
                scales=scales_of[b][:, columns],
                in_=grouped_of[b][:, first:last].rearrange("p j k t -> p (j k t)"),
            )

        def copy(on_vector, out, in_):
            if on_vector:
                nc.vector.tensor_copy(out=out, in_=in_)
            else:
                nc.scalar.copy(out=out, in_=in_)

        def leave(b, scalar_is_free):
            grouped = grouped_pool.tile([P, ROW_TILES, P, PACK], BF16, align_bytes=64, name="grouped")
            grouped_of[b] = grouped
            codes_of[b] = mx_pool.tile([P, ROW_TILES * P], U32, align_bytes=64, name="codes")
            scales_of[b] = mx_pool.tile([P, ROW_TILES * P], U8, align_bytes=64, name="scales")
            for j in range(TILES):
                nc.vector.tensor_tensor(
                    out=grouped[:, j],
                    in0=turned_of[b, j][:].rearrange("p t k -> p k t"),
                    in1=gain[:].unsqueeze(1).to_broadcast([P, P, PACK]),
                    op=ALU.mult,
                )
                if b == B - 1 and j == 1:
                    quantise(b, 0, 2)
            copy(
                not scalar_is_free,
                out=grouped[:, TILES].rearrange("p k t -> p (k t)").bitcast(F32)
                .rearrange("p (k u) -> p k u", u=2),
                in_=words_of[b][:].rearrange("p u k -> p k u"),
            )

        def product(out, b, j, first):
            rows = slice(j * P, (j + 1) * P)
            nc.tensor.matmul_mx(
                out=out,
                lhsT=codes_of[b][:, rows].bitcast(FP8X4),
                lhsT_scale=scales_of[b][:, rows],
                rhs=w_codes[:, first : 2 * D].bitcast(FP8X4),
                rhs_scale=w_scales[:, first : 2 * D],
                start=True,
                stop=True,
            )

        def multiply(b):
            for j in range(TILES):
                acc_of[b, j] = acc_psum.tile([P, 2 * D], F32, name="acc")
                product(acc_of[b, j][:], b, j, 0)
            acc_of[b, TILES] = acc_psum.tile([P, D], F32, name="acc")
            product(acc_of[b, TILES][:], b, TILES, D)

        def store_tile(b, j):
            nc.sync.dma_start(out=tokens(out_0[b])[:, j, :], in_=qk_of[b][:, 0, j])
            nc.sync.dma_start(out=tokens(out_1[b, 0:S, :])[:, j, :], in_=qk_of[b][:, 1, j])

        def store_memory(b):
            nc.sync.dma_start(out=out_1[b, S : S + P, :], in_=k_mem_of[b][:])

        def copy_out(b, scalar_is_free):
            qk = result_pool.tile([P, 2, TILES, D], F32, name="qk")
            qk_of[b] = qk
            vector_tile = b >= B - SHARED_TAIL if scalar_is_free else b % 2 == 0
            vector_memory = not scalar_is_free and b % 2 == 1
            for j in range(TILES):
                source = acc_of[b, j][:].rearrange("p (m d) -> p m d", m=2)
                if b == B - 1:
                    copy(False, out=qk[:, 0, j, :], in_=source[:, 0, :])
                    copy(True, out=qk[:, 1, j, :], in_=source[:, 1, :])
                else:
                    copy(vector_tile and j == TILES - 1, out=qk[:, :, j, :], in_=source)
                if b >= B - FINE_STORES:
                    store_tile(b, j)
                if j == 0 and b + SQUARES_AHEAD < B:
                    root(b + SQUARES_AHEAD)
            k_mem_of[b] = result_pool.tile([P, D], F32, name="k_mem")
            copy(vector_memory, out=k_mem_of[b][:], in_=acc_of[b, TILES][:])
            if b >= B - FINE_STORES:
                store_memory(b)

        def store(b):
            nc.sync.dma_start(out=tokens(out_0[b]), in_=qk_of[b][:, 0])
            nc.sync.dma_start(out=tokens(out_1[b, 0:S, :]), in_=qk_of[b][:, 1])
            store_memory(b)

        w_grouped = keep.tile([P, 2 * D, PACK], BF16, align_bytes=64)
        w_codes = keep.tile([P, 2 * D], U32, align_bytes=64)
        w_scales = keep.tile([P, 2 * D], U8, align_bytes=64)

        def prepare_weights():
            w_words = w_grouped[:].rearrange("p c t -> p (c t)").bitcast(F32)
            for m in range(2):
                w_turned = turned_psum.tile([P, 2, D], F32, name="turned")
                for repeat in range(4 if m == 0 else 1):
                    keep_busy(w_turned[:].rearrange("p u c -> p (u c)"), BUSY_COLUMNS_FIRST)
                for r in range(2):
                    for u in range(2):
                        nc.tensor.transpose(
                            w_turned[:, u, r * P : (r + 1) * P],
                            word_columns(w_raw[:, m, r, :], u),
                            ident[:],
                        )
                nc.vector.tensor_copy(
                    out=w_words[:, m * 2 * D : (m + 1) * 2 * D].rearrange("p (c u) -> p c u", u=2),
                    in_=w_turned[:].rearrange("p u c -> p c u"),
                )
            nc.vector.quantize_mx(
                out=w_codes[:].bitcast(FP8X4),
                scales=w_scales[:],
                in_=w_grouped[:].rearrange("p c t -> p (c t)"),
            )

        squares(0)
        root(0)
        reciprocal(0)
        scale(0)
        prepare_weights()
        for step in range(1 - SQUARES_AHEAD, B):
            scalar_is_free = step + SQUARES_AHEAD >= B
            if not scalar_is_free:
                squares(step + SQUARES_AHEAD)
                if step < 0:
                    root(step + SQUARES_AHEAD)
            if 2 <= step + SCALE_AHEAD < B:
                scale(step + SCALE_AHEAD)
            if 0 <= step + LEAVE_AHEAD < B:
                turn(step + LEAVE_AHEAD)
                if step + LEAVE_AHEAD == 0:
                    reciprocal(1)
                    scale(1)
                leave(step + LEAVE_AHEAD, scalar_is_free)
            if step >= 0:
                multiply(step)
                copy_out(step, scalar_is_free)
            if 2 <= step + RECIPROCAL_AHEAD < B:
                reciprocal(step + RECIPROCAL_AHEAD)
            if 0 <= step + LEAVE_AHEAD < B:
                quantise(step + LEAVE_AHEAD, 0 if step + LEAVE_AHEAD < B - 1 else 2, ROW_TILES)
            if 0 <= step < B - FINE_STORES:
                store(step)
